import numpy as np
import ml_dtypes


def mxq(x, axis, fmt="e4m3"):
    dtype, down = {"e4m3": (ml_dtypes.float8_e4m3fn, 7), "e5m2": (ml_dtypes.float8_e5m2, 14)}[fmt]
    v = np.moveaxis(np.asarray(x, np.float32).astype(ml_dtypes.bfloat16).astype(np.float64), axis, -1)
    blocks = v.reshape(v.shape[:-1] + (-1, 32))
    amax = np.abs(blocks).max(-1, keepdims=True)
    byte = np.maximum(np.where(amax > 0, np.frexp(amax)[1] - 1 + 127, 0) - down, 1)
    scale = np.exp2(byte - 127.0)
    codes = (blocks / scale).astype(np.float32).astype(dtype).astype(np.float64)
    return np.moveaxis((codes * scale).reshape(v.shape), -1, axis)


WIDE = False


def mx_kscale(k):
    if not WIDE:
        return np.ones(k)
    levels = np.array([10, -10, 5, -5, 0])
    a = np.random.permutation(np.resize(levels, k // 512 * 4)).reshape(k // 512, 4)
    idx = np.arange(k)
    return np.exp2(a[idx // 512, idx % 128 // 32])


BF16 = ml_dtypes.bfloat16


def bf(x):
    return np.asarray(x, np.float32).astype(BF16)


def f64(x):
    return np.asarray(x).astype(np.float64)


E2M1 = np.array([0.0, 0.5, 1.0, 1.5, 2.0, 3.0, 4.0, 6.0, -0.0, -0.5, -1.0, -1.5, -2.0, -3.0, -4.0, -6.0])


def pack_weight(w, fmt):
    k, n = w.shape
    w = f64(bf(w)).reshape(k // 32, 32, n)
    amax = np.abs(w).max(1)
    if fmt == "e4m3":
        byte = np.frexp(amax)[1] - 1 + 127 - 7
    else:
        mant, ex = np.frexp(amax / 6.0)
        byte = np.where(mant > 0.5, ex, ex - 1) + 127
    byte = np.clip(np.where(amax > 0, byte, 1), 1, 254)
    scaled = (w * np.exp2(127.0 - byte)[:, None, :]).reshape(k, n).astype(np.float32)
    by_word = np.ascontiguousarray(scaled.reshape(k // 512, 128, 4, n).transpose(0, 1, 3, 2))
    if fmt == "e4m3":
        words = by_word.astype(ml_dtypes.float8_e4m3fn).view(np.uint8)
    else:
        c = by_word.astype(ml_dtypes.float4_e2m1fn).view(np.uint8) & 0xF
        words = c[..., 0::2] | (c[..., 1::2] << 4)
    return np.ascontiguousarray(words), np.ascontiguousarray(byte.astype(np.uint8).reshape(k // 512, 16, n))


def unpack_weight(words, scales, fmt):
    g, p, n, _ = words.shape
    if fmt == "e4m3":
        vals = np.ascontiguousarray(words).view(ml_dtypes.float8_e4m3fn).astype(np.float64)
    else:
        nib = np.empty((g, p, n, 4), np.uint8)
        nib[..., 0::2] = words & 0xF
        nib[..., 1::2] = words >> 4
        vals = E2M1[nib]
    vals = vals * np.repeat(np.exp2(scales.astype(np.float64) - 127.0), 8, axis=1)[..., None]
    return vals.transpose(0, 1, 3, 2).reshape(g * 512, n)


B, CIN, COUT, H, W = 2, 4096, 4096, 8, 8


def setup_inputs():
    s = mx_kscale(CIN)
    x = np.random.standard_normal((B, CIN, H, W)) * s[None, :, None, None]
    weight = np.random.uniform(-1.0, 1.0, (CIN, COUT)) * np.sqrt(3.0 / CIN) / s[:, None]
    words, scales = pack_weight(weight, "e4m3")
    return {"x": bf(x), "weight_words": words, "weight_scales": scales}


def reference(x, weight_words, weight_scales):
    wq = unpack_weight(weight_words, weight_scales, "e4m3")
    xq = mxq(f64(x), 1, "e4m3")
    return np.einsum("io,bihw->bohw", wq, xq, optimize=True)

@@ -1,0 +1,145 @@
+from contextlib import ExitStack
+
+import concourse.mybir as mybir
+from concourse.masks import make_identity
+
+F32 = mybir.dt.float32
+BF16 = mybir.dt.bfloat16
+I32 = mybir.dt.int32
+U32 = mybir.dt.uint32
+U8 = mybir.dt.uint8
+FP8X4 = mybir.dt.float8_e4m3fn_x4
+
+P = 128
+G = 8
+NB = 512
+TOK = 128
+J = 4
+COUT = 4096
+FLOPS = 2 * TOK * 4096 * COUT
+
+CHUNK_BANKS = [[0, 1, 2, 3], [4, 5, 6, 7]]
+LOADS_AHEAD = 4
+
+
+def tile_simpleconvolution_w_kernel(tc, x, weight_words, weight_scales, out):
+    nc = tc.nc
+    with ExitStack() as ctx:
+        keep = ctx.enter_context(tc.tile_pool(name="keep", bufs=1))
+        s1_pool = ctx.enter_context(tc.tile_pool(name="s1", bufs=4))
+        o_pool = ctx.enter_context(tc.tile_pool(name="o", bufs=4))
+        psum = ctx.enter_context(tc.psum_pool(name="ps", bufs=1))
+        ctx.enter_context(tc.manual_schedule())
+
+        ident = keep.tile([P, P], F32, name="ident")
+        make_identity(nc, ident[:])
+
+        planes = []
+        for c in range(2):
+            pl = keep.tile([P, COUT], U8, name="planes%d" % c, align_bytes=64)
+            nc.vector.memset(pl[:].bitcast(I32), 0)
+            planes.append(pl)
+
+        xb = []
+        for b in range(2):
+            t = keep.tile([P, G, 256], BF16, name="xb%d" % b)
+            nc.scalar.dma_start(
+                out=t[:], in_=x[b].rearrange("(g p t) h w -> p g (t h w)", g=G, p=P, t=4)
+            )
+            xb.append(t)
+
+        def load_w(g, c0, c1):
+            t = keep.tile([P, c1 - c0], I32, name="w%d_%d" % (g, c0), align_bytes=64)
+            src = weight_words[g].rearrange("p n t -> p (n t)")[:, 4 * c0 : 4 * c1]
+            nc.sync.dma_start(out=t[:], in_=src.bitcast(I32))
+            return t
+
+        def load_scales(c):
+            for q in range(4):
+                nc.sync.dma_start(
+                    out=planes[c][32 * q : 32 * q + 16, :].bitcast(I32),
+                    in_=weight_scales[4 * c : 4 * c + 4, 4 * q : 4 * q + 4, :].bitcast(I32),
+                )
+
+        where = {}
+
+        def load_chunk_g(banks, g, split):
+            if split:
+                for bk in banks:
+                    where[(g, bk)] = (load_w(g, NB * bk, NB * bk + NB), 0)
+            else:
+                t = load_w(g, NB * banks[0], NB * banks[-1] + NB)
+                for i, bk in enumerate(banks):
+                    where[(g, bk)] = (t, NB * i)
+
+        first = CHUNK_BANKS[0]
+        load_chunk_g(first, 0, False)
+        load_scales(0)
+        load_chunk_g(first, 1, False)
+        load_chunk_g(first, 2, False)
+        load_scales(1)
+        for g in range(3, G):
+            load_chunk_g(first, g, len(CHUNK_BANKS) == 1 and g == G - 1)
+
+        grouped = keep.tile([P, G, TOK, 4], BF16, name="grouped", align_bytes=64)
+        x_codes = keep.tile([P, G * TOK], U32, name="x_codes", align_bytes=64)
+        x_plane = keep.tile([P, G * TOK], U8, name="x_plane", align_bytes=64)
+        nc.vector.tensor_copy(
+            out=grouped[:, :, 0:64, :], in_=xb[0][:].rearrange("p g (t s) -> p g s t", t=4)
+        )
+        nc.scalar.copy(
+            out=grouped[:, :, 64:128, :], in_=xb[1][:].rearrange("p g (t s) -> p g s t", t=4)
+        )
+        nc.vector.quantize_mx(
+            out=x_codes[:].bitcast(FP8X4),
+            scales=x_plane[:],
+            in_=grouped[:].rearrange("p g k t -> p (g k t)"),
+        )
+
+        out_v = out.rearrange("b (c m j) h w -> c m b (j h w)", c=COUT // NB, m=P, j=J)
+
+        def copy_on(e, dst, src):
+            if e % 2 == 0:
+                nc.vector.tensor_copy(out=dst, in_=src)
+            else:
+                nc.scalar.copy(out=dst, in_=src)
+
+        for ci, banks in enumerate(CHUNK_BANKS):
+            last_chunk = ci == len(CHUNK_BANKS) - 1
+            if not last_chunk:
+                nxt = CHUNK_BANKS[ci + 1]
+                nxt_last = ci + 1 == len(CHUNK_BANKS) - 1
+                for g in range(LOADS_AHEAD):
+                    load_chunk_g(nxt, g, False)
+            acc = {}
+            for bk in banks:
+                acc[bk] = psum.tile([P, NB], F32, name="acc%d" % bk, tag="bank%d" % bk)
+            for g in range(G):
+                k = 4 * (g % 4)
+                for bk in banks:
+                    wt, off = where[(g, bk)]
+                    nc.tensor.matmul_mx(
+                        out=acc[bk][:],
+                        lhsT=x_codes[:, TOK * g : TOK * g + TOK].bitcast(FP8X4),
+                        lhsT_scale=x_plane[:, TOK * g : TOK * g + TOK],
+                        rhs=wt[:, off : off + NB].bitcast(FP8X4),
+                        rhs_scale=planes[g // 4][k:P, NB * bk : NB * bk + NB],
+                        start=(g == 0),
+                        stop=(g == G - 1),
+                    )
+            s1 = {}
+            for i, bk in enumerate(banks):
+                s1[bk] = s1_pool.tile([P, J, P], F32, name="s1")
+                copy_on(i, s1[bk][:], acc[bk][:].rearrange("p (m j) -> p j m", j=J))
+            tp = {}
+            for bk in banks:
+                tp[bk] = psum.tile([P, J, TOK], F32, name="tp%d" % bk, tag="bank%d" % bk)
+                for j in range(J):
+                    nc.tensor.transpose(tp[bk][:, j, :], s1[bk][:, j, :], ident[:])
+            for i, bk in enumerate(banks):
+                o_sb = o_pool.tile([P, 2, J, 64], F32, name="o_sb")
+                copy_on(i, o_sb[:], tp[bk][:].rearrange("p j (b s) -> p b j s", b=2))
+                nc.sync.dma_start(out=out_v[bk], in_=o_sb[:].rearrange("p b j s -> p b (j s)"))
+            if not last_chunk:
+                for g in range(LOADS_AHEAD, G):
+                    load_chunk_g(nxt, g, nxt_last and g == G - 1)

@@ -14,25 +14,19 @@ P = 128
 G = 8
 NB = 512
 TOK = 128
-J = 4
 COUT = 4096
 FLOPS = 2 * TOK * 4096 * COUT
 
-CHUNK_BANKS = [[0, 1, 2, 3], [4, 5, 6, 7]]
-LOADS_AHEAD = 4
+CHUNKS = [([0, 1, 2, 3], [[0, 1, 2, 3]]), ([4, 5, 6, 7], [[4], [5], [6], [7]])]
+SCALES_ON_GPSIMD = False
 
 
 def tile_simpleconvolution_w_kernel(tc, x, weight_words, weight_scales, out):
     nc = tc.nc
     with ExitStack() as ctx:
         keep = ctx.enter_context(tc.tile_pool(name="keep", bufs=1))
-        s1_pool = ctx.enter_context(tc.tile_pool(name="s1", bufs=4))
-        o_pool = ctx.enter_context(tc.tile_pool(name="o", bufs=4))
         psum = ctx.enter_context(tc.psum_pool(name="ps", bufs=1))
         ctx.enter_context(tc.manual_schedule())
-
-        ident = keep.tile([P, P], F32, name="ident")
-        make_identity(nc, ident[:])
 
         planes = []
         for c in range(2):
@@ -56,30 +50,35 @@ def tile_simpleconvolution_w_kernel(tc, x, weight_words, weight_scales, out):
 
         def load_scales(c):
             for q in range(4):
-                nc.sync.dma_start(
-                    out=planes[c][32 * q : 32 * q + 16, :].bitcast(I32),
-                    in_=weight_scales[4 * c : 4 * c + 4, 4 * q : 4 * q + 4, :].bitcast(I32),
-                )
+                dst = planes[c][32 * q : 32 * q + 16, :]
+                src = weight_scales[4 * c : 4 * c + 4, 4 * q : 4 * q + 4, :]
+                if SCALES_ON_GPSIMD:
+                    nc.gpsimd.dma_start(out=dst.bitcast(F32), in_=src.bitcast(F32))
+                else:
+                    nc.sync.dma_start(out=dst.bitcast(I32), in_=src.bitcast(I32))
+
+        if SCALES_ON_GPSIMD:
+            load_scales(0)
+            load_scales(1)
+
+        ident = keep.tile([P, P], F32, name="ident")
+        make_identity(nc, ident[:])
 
         where = {}
-
-        def load_chunk_g(banks, g, split):
-            if split:
-                for bk in banks:
-                    where[(g, bk)] = (load_w(g, NB * bk, NB * bk + NB), 0)
-            else:
-                t = load_w(g, NB * banks[0], NB * banks[-1] + NB)
-                for i, bk in enumerate(banks):
-                    where[(g, bk)] = (t, NB * i)
-
-        first = CHUNK_BANKS[0]
-        load_chunk_g(first, 0, False)
-        load_scales(0)
-        load_chunk_g(first, 1, False)
-        load_chunk_g(first, 2, False)
-        load_scales(1)
-        for g in range(3, G):
-            load_chunk_g(first, g, len(CHUNK_BANKS) == 1 and g == G - 1)
+        for ci, (banks, groups) in enumerate(CHUNKS):
+            for g in range(G):
+                if ci == len(CHUNKS) - 1 and g == G - 1:
+                    for bk in banks:
+                        where[(g, bk)] = (load_w(g, NB * bk, NB * bk + NB), 0)
+                else:
+                    t = load_w(g, NB * banks[0], NB * banks[-1] + NB)
+                    for i, bk in enumerate(banks):
+                        where[(g, bk)] = (t, NB * i)
+                if ci == 0 and not SCALES_ON_GPSIMD:
+                    if g == 0:
+                        load_scales(0)
+                    if g == 2:
+                        load_scales(1)
 
         grouped = keep.tile([P, G, TOK, 4], BF16, name="grouped", align_bytes=64)
         x_codes = keep.tile([P, G * TOK], U32, name="x_codes", align_bytes=64)
@@ -96,7 +95,7 @@ def tile_simpleconvolution_w_kernel(tc, x, weight_words, weight_scales, out):
             in_=grouped[:].rearrange("p g k t -> p (g k t)"),
         )
 
-        out_v = out.rearrange("b (c m j) h w -> c m b (j h w)", c=COUT // NB, m=P, j=J)
+        out_f = out.rearrange("b o h w -> b o (h w)")
 
         def copy_on(e, dst, src):
             if e % 2 == 0:
@@ -104,13 +103,7 @@ def tile_simpleconvolution_w_kernel(tc, x, weight_words, weight_scales, out):
             else:
                 nc.scalar.copy(out=dst, in_=src)
 
-        for ci, banks in enumerate(CHUNK_BANKS):
-            last_chunk = ci == len(CHUNK_BANKS) - 1
-            if not last_chunk:
-                nxt = CHUNK_BANKS[ci + 1]
-                nxt_last = ci + 1 == len(CHUNK_BANKS) - 1
-                for g in range(LOADS_AHEAD):
-                    load_chunk_g(nxt, g, False)
+        for banks, groups in CHUNKS:
             acc = {}
             for bk in banks:
                 acc[bk] = psum.tile([P, NB], F32, name="acc%d" % bk, tag="bank%d" % bk)
@@ -128,18 +121,40 @@ def tile_simpleconvolution_w_kernel(tc, x, weight_words, weight_scales, out):
                         stop=(g == G - 1),
                     )
             s1 = {}
-            for i, bk in enumerate(banks):
-                s1[bk] = s1_pool.tile([P, J, P], F32, name="s1")
-                copy_on(i, s1[bk][:], acc[bk][:].rearrange("p (m j) -> p j m", j=J))
+            e = 0
+            for grp in groups:
+                nb = len(grp)
+                jg = 4 * nb
+                mc = P // nb
+                s1[grp[0]] = keep.tile([P, jg, P], F32, name="s1_%d" % grp[0])
+                for i, bk in enumerate(grp):
+                    copy_on(
+                        e,
+                        s1[grp[0]][:, :, mc * i : mc * i + mc],
+                        acc[bk][:].rearrange("p (m j) -> p j m", j=jg),
+                    )
+                    e += 1
             tp = {}
-            for bk in banks:
-                tp[bk] = psum.tile([P, J, TOK], F32, name="tp%d" % bk, tag="bank%d" % bk)
-                for j in range(J):
-                    nc.tensor.transpose(tp[bk][:, j, :], s1[bk][:, j, :], ident[:])
-            for i, bk in enumerate(banks):
-                o_sb = o_pool.tile([P, 2, J, 64], F32, name="o_sb")
-                copy_on(i, o_sb[:], tp[bk][:].rearrange("p j (b s) -> p b j s", b=2))
-                nc.sync.dma_start(out=out_v[bk], in_=o_sb[:].rearrange("p b j s -> p b (j s)"))
-            if not last_chunk:
-                for g in range(LOADS_AHEAD, G):
-                    load_chunk_g(nxt, g, nxt_last and g == G - 1)
+            for grp in groups:
+                for i, bk in enumerate(grp):
+                    tp[bk] = psum.tile([P, 4, TOK], F32, name="tp%d" % bk, tag="bank%d" % bk)
+                    for j in range(4):
+                        nc.tensor.transpose(tp[bk][:, j, :], s1[grp[0]][:, 4 * i + j, :], ident[:])
+            e = 0
+            for grp in groups:
+                jg = 4 * len(grp)
+                o_sb = keep.tile([P, 2, jg, 64], F32, name="o_%d" % grp[0])
+                for i, bk in enumerate(grp):
+                    copy_on(
+                        e,
+                        o_sb[:, :, 4 * i : 4 * i + 4, :],
+                        tp[bk][:].rearrange("p j (b s) -> p b j s", b=2),
+                    )
+                    e += 1
+                base = NB * grp[0]
+                nc.sync.dma_start(
+                    out=out_f[:, base : base + NB * len(grp), :].rearrange(
+                        "b (m j) s -> m b (j s)", j=jg
+                    ),
+                    in_=o_sb[:].rearrange("p b j s -> p b (j s)"),
+                )

@@ -18,7 +18,7 @@ COUT = 4096
 FLOPS = 2 * TOK * 4096 * COUT
 
 CHUNKS = [([0, 1, 2, 3], [[0, 1, 2, 3]]), ([4, 5, 6, 7], [[4], [5], [6], [7]])]
-SCALES_ON_GPSIMD = False
+SCALES_ON_GPSIMD = True
 
 
 def tile_simpleconvolution_w_kernel(tc, x, weight_words, weight_scales, out):

@@ -17,8 +17,17 @@ TOK = 128
 COUT = 4096
 FLOPS = 2 * TOK * 4096 * COUT
 
-CHUNKS = [([0, 1, 2, 3], [[0, 1, 2, 3]]), ([4, 5, 6, 7], [[4], [5], [6], [7]])]
-SCALES_ON_GPSIMD = True
+ALL = [0, 1, 2, 3, 4, 5, 6, 7]
+HALF_A = [0, 1, 2, 3]
+HALF_B = [4, 5, 6, 7]
+FULL_G = 4
+UNITS = (
+    [(g, ALL) for g in range(FULL_G)]
+    + [(g, HALF_A) for g in range(FULL_G, G)]
+    + [(g, HALF_B) for g in range(FULL_G, G - 1)]
+    + [(G - 1, [bk]) for bk in HALF_B]
+)
+STORE_GROUPS = {FULL_G + (G - FULL_G) - 1: [HALF_A], len(UNITS) - 1: [[4], [5], [6], [7]]}
 
 
 def tile_simpleconvolution_w_kernel(tc, x, weight_words, weight_scales, out):
@@ -42,43 +51,24 @@ def tile_simpleconvolution_w_kernel(tc, x, weight_words, weight_scales, out):
             )
             xb.append(t)
 
-        def load_w(g, c0, c1):
-            t = keep.tile([P, c1 - c0], I32, name="w%d_%d" % (g, c0), align_bytes=64)
-            src = weight_words[g].rearrange("p n t -> p (n t)")[:, 4 * c0 : 4 * c1]
-            nc.sync.dma_start(out=t[:], in_=src.bitcast(I32))
-            return t
-
-        def load_scales(c):
+        for c in range(2):
             for q in range(4):
-                dst = planes[c][32 * q : 32 * q + 16, :]
-                src = weight_scales[4 * c : 4 * c + 4, 4 * q : 4 * q + 4, :]
-                if SCALES_ON_GPSIMD:
-                    nc.gpsimd.dma_start(out=dst.bitcast(F32), in_=src.bitcast(F32))
-                else:
-                    nc.sync.dma_start(out=dst.bitcast(I32), in_=src.bitcast(I32))
-
-        if SCALES_ON_GPSIMD:
-            load_scales(0)
-            load_scales(1)
+                nc.gpsimd.dma_start(
+                    out=planes[c][32 * q : 32 * q + 16, :].bitcast(F32),
+                    in_=weight_scales[4 * c : 4 * c + 4, 4 * q : 4 * q + 4, :].bitcast(F32),
+                )
 
         ident = keep.tile([P, P], F32, name="ident")
         make_identity(nc, ident[:])
 
-        where = {}
-        for ci, (banks, groups) in enumerate(CHUNKS):
-            for g in range(G):
-                if ci == len(CHUNKS) - 1 and g == G - 1:
-                    for bk in banks:
-                        where[(g, bk)] = (load_w(g, NB * bk, NB * bk + NB), 0)
-                else:
-                    t = load_w(g, NB * banks[0], NB * banks[-1] + NB)
-                    for i, bk in enumerate(banks):
-                        where[(g, bk)] = (t, NB * i)
-                if ci == 0 and not SCALES_ON_GPSIMD:
-                    if g == 0:
-                        load_scales(0)
-                    if g == 2:
-                        load_scales(1)
+        w_tiles = []
+        for g, banks in UNITS:
+            c0 = NB * banks[0]
+            c1 = NB * banks[-1] + NB
+            t = keep.tile([P, c1 - c0], I32, name="w%d_%d" % (g, c0), align_bytes=64)
+            src = weight_words[g].rearrange("p n t -> p (n t)")[:, 4 * c0 : 4 * c1]
+            nc.sync.dma_start(out=t[:], in_=src.bitcast(I32))
+            w_tiles.append(t)
 
         grouped = keep.tile([P, G, TOK, 4], BF16, name="grouped", align_bytes=64)
         x_codes = keep.tile([P, G * TOK], U32, name="x_codes", align_bytes=64)
@@ -103,23 +93,11 @@ def tile_simpleconvolution_w_kernel(tc, x, weight_words, weight_scales, out):
             else:
                 nc.scalar.copy(out=dst, in_=src)
 
-        for banks, groups in CHUNKS:
-            acc = {}
-            for bk in banks:
-                acc[bk] = psum.tile([P, NB], F32, name="acc%d" % bk, tag="bank%d" % bk)
-            for g in range(G):
-                k = 4 * (g % 4)
-                for bk in banks:
-                    wt, off = where[(g, bk)]
-                    nc.tensor.matmul_mx(
-                        out=acc[bk][:],
-                        lhsT=x_codes[:, TOK * g : TOK * g + TOK].bitcast(FP8X4),
-                        lhsT_scale=x_plane[:, TOK * g : TOK * g + TOK],
-                        rhs=wt[:, off : off + NB].bitcast(FP8X4),
-                        rhs_scale=planes[g // 4][k:P, NB * bk : NB * bk + NB],
-                        start=(g == 0),
-                        stop=(g == G - 1),
-                    )
+        acc = {}
+        for bk in ALL:
+            acc[bk] = psum.tile([P, NB], F32, name="acc%d" % bk, tag="bank%d" % bk)
+
+        def leave_psum(groups):
             s1 = {}
             e = 0
             for grp in groups:
@@ -158,3 +136,18 @@ def tile_simpleconvolution_w_kernel(tc, x, weight_words, weight_scales, out):
                     ),
                     in_=o_sb[:].rearrange("p b j s -> p b (j s)"),
                 )
+
+        for u, (g, banks) in enumerate(UNITS):
+            k = 4 * (g % 4)
+            for i, bk in enumerate(banks):
+                nc.tensor.matmul_mx(
+                    out=acc[bk][:],
+                    lhsT=x_codes[:, TOK * g : TOK * g + TOK].bitcast(FP8X4),
+                    lhsT_scale=x_plane[:, TOK * g : TOK * g + TOK],
+                    rhs=w_tiles[u][:, NB * i : NB * i + NB].bitcast(FP8X4),
+                    rhs_scale=planes[g // 4][k:P, NB * bk : NB * bk + NB],
+                    start=(g == 0),
+                    stop=(g == G - 1),
+                )
+            if u in STORE_GROUPS:
+                leave_psum(STORE_GROUPS[u])

@@ -24,10 +24,10 @@ FULL_G = 4
 UNITS = (
     [(g, ALL) for g in range(FULL_G)]
     + [(g, HALF_A) for g in range(FULL_G, G)]
-    + [(g, HALF_B) for g in range(FULL_G, G - 1)]
-    + [(G - 1, [bk]) for bk in HALF_B]
+    + [(g, HALF_B) for g in range(FULL_G, G - 2)]
+    + [(G - 2, [4, 5]), (G - 1, [4, 5]), (G - 2, [6, 7]), (G - 1, [6]), (G - 1, [7])]
 )
-STORE_GROUPS = {FULL_G + (G - FULL_G) - 1: [HALF_A], len(UNITS) - 1: [[4], [5], [6], [7]]}
+STORE_GROUPS = {FULL_G + (G - FULL_G) - 1: [HALF_A], len(UNITS) - 1: [[4, 5], [6, 7]]}
 
 
 def tile_simpleconvolution_w_kernel(tc, x, weight_words, weight_scales, out):

@@ -43,13 +43,11 @@ def tile_simpleconvolution_w_kernel(tc, x, weight_words, weight_scales, out):
             nc.vector.memset(pl[:].bitcast(I32), 0)
             planes.append(pl)
 
-        xb = []
-        for b in range(2):
-            t = keep.tile([P, G, 256], BF16, name="xb%d" % b)
-            nc.scalar.dma_start(
-                out=t[:], in_=x[b].rearrange("(g p t) h w -> p g (t h w)", g=G, p=P, t=4)
-            )
-            xb.append(t)
+        xr = keep.tile([P, 2, 2048], BF16, name="xr")
+        nc.sync.dma_start(out=xr[:], in_=x.rearrange("b (q i) h w -> q b (i h w)", i=32))
+
+        ident = keep.tile([P, P], F32, name="ident")
+        make_identity(nc, ident[:])
 
         for c in range(2):
             for q in range(4):
@@ -57,9 +55,6 @@ def tile_simpleconvolution_w_kernel(tc, x, weight_words, weight_scales, out):
                     out=planes[c][32 * q : 32 * q + 16, :].bitcast(F32),
                     in_=weight_scales[4 * c : 4 * c + 4, 4 * q : 4 * q + 4, :].bitcast(F32),
                 )
-
-        ident = keep.tile([P, P], F32, name="ident")
-        make_identity(nc, ident[:])
 
         w_tiles = []
         for g, banks in UNITS:
@@ -73,12 +68,39 @@ def tile_simpleconvolution_w_kernel(tc, x, weight_words, weight_scales, out):
         grouped = keep.tile([P, G, TOK, 4], BF16, name="grouped", align_bytes=64)
         x_codes = keep.tile([P, G * TOK], U32, name="x_codes", align_bytes=64)
         x_plane = keep.tile([P, G * TOK], U8, name="x_plane", align_bytes=64)
-        nc.vector.tensor_copy(
-            out=grouped[:, :, 0:64, :], in_=xb[0][:].rearrange("p g (t s) -> p g s t", t=4)
-        )
-        nc.scalar.copy(
-            out=grouped[:, :, 64:128, :], in_=xb[1][:].rearrange("p g (t s) -> p g s t", t=4)
-        )
+
+        def copy_on(e, dst, src):
+            if e % 2 == 0:
+                nc.vector.tensor_copy(out=dst, in_=src)
+            else:
+                nc.scalar.copy(out=dst, in_=src)
+
+        xw = xr[:].bitcast(F32)
+        turned = keep.tile([P, 2, P, 8], F32, name="turned")
+        for b in range(2):
+            for half in range(2):
+                t1 = psum.tile([P, 4, P], F32, name="t1_%d%d" % (b, half), tag="bank%d" % (2 * b + half))
+                for i in range(4):
+                    c0 = P * (4 * half + i)
+                    nc.tensor.transpose(t1[:, i, :], xw[:, b, c0 : c0 + P], ident[:])
+                copy_on(
+                    b, turned[:, b, :, 4 * half : 4 * half + 4], t1[:].rearrange("c i q -> c q i")
+                )
+        for b in range(2):
+            for half in range(2):
+                t2 = psum.tile([P, 4, P], F32, name="t2_%d%d" % (b, half), tag="bank%d" % (4 + 2 * b + half))
+                for i in range(4):
+                    g = 4 * half + i
+                    nc.tensor.transpose(
+                        t2[:, i, :],
+                        turned[:, b, 16 * g : 16 * g + 16, :].rearrange("c h l -> c (h l)"),
+                        ident[:],
+                    )
+                copy_on(
+                    b,
+                    grouped[:, 4 * half : 4 * half + 4, 64 * b : 64 * b + 64, :],
+                    t2[:].bitcast(BF16).rearrange("p g (t s) -> p g s t", t=4),
+                )
         nc.vector.quantize_mx(
             out=x_codes[:].bitcast(FP8X4),
             scales=x_plane[:],
@@ -86,12 +108,6 @@ def tile_simpleconvolution_w_kernel(tc, x, weight_words, weight_scales, out):
         )
 
         out_f = out.rearrange("b o h w -> b o (h w)")
-
-        def copy_on(e, dst, src):
-            if e % 2 == 0:
-                nc.vector.tensor_copy(out=dst, in_=src)
-            else:
-                nc.scalar.copy(out=dst, in_=src)
 
         acc = {}
         for bk in ALL:

@@ -15,19 +15,13 @@ G = 8
 NB = 512
 TOK = 128
 COUT = 4096
+MB = 128
 FLOPS = 2 * TOK * 4096 * COUT
 
-ALL = [0, 1, 2, 3, 4, 5, 6, 7]
-HALF_A = [0, 1, 2, 3]
-HALF_B = [4, 5, 6, 7]
 FULL_G = 4
-UNITS = (
-    [(g, ALL) for g in range(FULL_G)]
-    + [(g, HALF_A) for g in range(FULL_G, G)]
-    + [(g, HALF_B) for g in range(FULL_G, G - 2)]
-    + [(G - 2, [4, 5]), (G - 1, [4, 5]), (G - 2, [6, 7]), (G - 1, [6]), (G - 1, [7])]
-)
-STORE_GROUPS = {FULL_G + (G - FULL_G) - 1: [HALF_A], len(UNITS) - 1: [[4, 5], [6, 7]]}
+XS_BANKS = [0, 1, 2, 3, 4, 5, 6]
+Q0 = NB * 7
+Q_BANK = [7, 0, 1, 2]
 
 
 def tile_simpleconvolution_w_kernel(tc, x, weight_words, weight_scales, out):
@@ -56,14 +50,23 @@ def tile_simpleconvolution_w_kernel(tc, x, weight_words, weight_scales, out):
                     in_=weight_scales[4 * c : 4 * c + 4, 4 * q : 4 * q + 4, :].bitcast(F32),
                 )
 
-        w_tiles = []
-        for g, banks in UNITS:
-            c0 = NB * banks[0]
-            c1 = NB * banks[-1] + NB
+        def load(g, c0, c1):
             t = keep.tile([P, c1 - c0], I32, name="w%d_%d" % (g, c0), align_bytes=64)
             src = weight_words[g].rearrange("p n t -> p (n t)")[:, 4 * c0 : 4 * c1]
             nc.sync.dma_start(out=t[:], in_=src.bitcast(I32))
-            w_tiles.append(t)
+            return t
+
+        w_a = [load(g, 0, 4 * NB) for g in range(G)]
+        w_b = [load(g, 4 * NB, COUT) for g in range(FULL_G)]
+        w_45 = [load(g, 4 * NB, 6 * NB) for g in range(FULL_G, G)]
+        w_6 = [load(g, 6 * NB, 7 * NB) for g in range(FULL_G, G)]
+        w_q = []
+        for first, nblk in ((0, 2), (2, 1), (3, 1)):
+            c0 = Q0 + MB * first
+            t = keep.tile([P, G - FULL_G, MB * nblk], I32, name="wq%d" % first, align_bytes=64)
+            src = weight_words[FULL_G:G].rearrange("g p n t -> p g (n t)")[:, :, 4 * c0 : 4 * (c0 + MB * nblk)]
+            nc.sync.dma_start(out=t[:], in_=src.bitcast(I32))
+            w_q.append((t, first, nblk))
 
         grouped = keep.tile([P, G, TOK, 4], BF16, name="grouped", align_bytes=64)
         x_codes = keep.tile([P, G * TOK], U32, name="x_codes", align_bytes=64)
@@ -110,60 +113,116 @@ def tile_simpleconvolution_w_kernel(tc, x, weight_words, weight_scales, out):
         out_f = out.rearrange("b o h w -> b o (h w)")
 
         acc = {}
-        for bk in ALL:
+        for bk in XS_BANKS:
             acc[bk] = psum.tile([P, NB], F32, name="acc%d" % bk, tag="bank%d" % bk)
 
-        def leave_psum(groups):
-            s1 = {}
-            e = 0
-            for grp in groups:
-                nb = len(grp)
-                jg = 4 * nb
-                mc = P // nb
-                s1[grp[0]] = keep.tile([P, jg, P], F32, name="s1_%d" % grp[0])
-                for i, bk in enumerate(grp):
-                    copy_on(
-                        e,
-                        s1[grp[0]][:, :, mc * i : mc * i + mc],
-                        acc[bk][:].rearrange("p (m j) -> p j m", j=jg),
-                    )
-                    e += 1
-            tp = {}
-            for grp in groups:
-                for i, bk in enumerate(grp):
-                    tp[bk] = psum.tile([P, 4, TOK], F32, name="tp%d" % bk, tag="bank%d" % bk)
-                    for j in range(4):
-                        nc.tensor.transpose(tp[bk][:, j, :], s1[grp[0]][:, 4 * i + j, :], ident[:])
-            e = 0
-            for grp in groups:
-                jg = 4 * len(grp)
-                o_sb = keep.tile([P, 2, jg, 64], F32, name="o_%d" % grp[0])
-                for i, bk in enumerate(grp):
-                    copy_on(
-                        e,
-                        o_sb[:, :, 4 * i : 4 * i + 4, :],
-                        tp[bk][:].rearrange("p j (b s) -> p b j s", b=2),
-                    )
-                    e += 1
-                base = NB * grp[0]
-                nc.sync.dma_start(
-                    out=out_f[:, base : base + NB * len(grp), :].rearrange(
-                        "b (m j) s -> m b (j s)", j=jg
-                    ),
-                    in_=o_sb[:].rearrange("p b j s -> p b (j s)"),
+        def pass_x(g, bk, wt, col):
+            k = 4 * (g % 4)
+            nc.tensor.matmul_mx(
+                out=acc[bk][:],
+                lhsT=x_codes[:, TOK * g : TOK * g + TOK].bitcast(FP8X4),
+                lhsT_scale=x_plane[:, TOK * g : TOK * g + TOK],
+                rhs=wt[:, col : col + NB].bitcast(FP8X4),
+                rhs_scale=planes[g // 4][k:P, NB * bk : NB * bk + NB],
+                start=(g == 0),
+                stop=(g == G - 1),
+            )
+
+        acc_q = {}
+
+        def pass_w(g, blk, w_ap):
+            k = 4 * (g % 4)
+            c0 = Q0 + MB * blk
+            nc.tensor.matmul_mx(
+                out=acc_q[blk][:],
+                lhsT=w_ap.bitcast(FP8X4),
+                lhsT_scale=planes[g // 4][k:P, c0 : c0 + MB],
+                rhs=x_codes[:, TOK * g : TOK * g + TOK].bitcast(FP8X4),
+                rhs_scale=x_plane[:, TOK * g : TOK * g + TOK],
+                start=(g == 0),
+                stop=(g == G - 1),
+            )
+
+        s1 = {}
+        tp = {}
+
+        def leave_1(grp, e):
+            nb = len(grp)
+            jg = 4 * nb
+            mc = P // nb
+            s1[grp[0]] = keep.tile([P, jg, P], F32, name="s1_%d" % grp[0])
+            for i, bk in enumerate(grp):
+                copy_on(
+                    e + i,
+                    s1[grp[0]][:, :, mc * i : mc * i + mc],
+                    acc[bk][:].rearrange("p (m j) -> p j m", j=jg),
                 )
 
-        for u, (g, banks) in enumerate(UNITS):
-            k = 4 * (g % 4)
-            for i, bk in enumerate(banks):
-                nc.tensor.matmul_mx(
-                    out=acc[bk][:],
-                    lhsT=x_codes[:, TOK * g : TOK * g + TOK].bitcast(FP8X4),
-                    lhsT_scale=x_plane[:, TOK * g : TOK * g + TOK],
-                    rhs=w_tiles[u][:, NB * i : NB * i + NB].bitcast(FP8X4),
-                    rhs_scale=planes[g // 4][k:P, NB * bk : NB * bk + NB],
-                    start=(g == 0),
-                    stop=(g == G - 1),
+        def leave_2(grp):
+            for i, bk in enumerate(grp):
+                tp[bk] = psum.tile([P, 4, TOK], F32, name="tp%d" % bk, tag="bank%d" % bk)
+                for j in range(4):
+                    nc.tensor.transpose(tp[bk][:, j, :], s1[grp[0]][:, 4 * i + j, :], ident[:])
+
+        def leave_3(grp, e):
+            jg = 4 * len(grp)
+            o_sb = keep.tile([P, 2, jg, 64], F32, name="o_%d" % grp[0])
+            for i, bk in enumerate(grp):
+                copy_on(
+                    e + i,
+                    o_sb[:, :, 4 * i : 4 * i + 4, :],
+                    tp[bk][:].rearrange("p j (b s) -> p b j s", b=2),
                 )
-            if u in STORE_GROUPS:
-                leave_psum(STORE_GROUPS[u])
+            base = NB * grp[0]
+            nc.sync.dma_start(
+                out=out_f[:, base : base + NB * len(grp), :].rearrange("b (m j) s -> m b (j s)", j=jg),
+                in_=o_sb[:].rearrange("p b j s -> p b (j s)"),
+            )
+
+        o_q = keep.tile([P, 4, 2, 64], F32, name="o_q")
+
+        def leave_q(blk, e):
+            copy_on(e, o_q[:, blk, :, :].rearrange("p b s -> p (b s)"), acc_q[blk][:])
+            c0 = Q0 + MB * blk
+            nc.sync.dma_start(
+                out=out_f[:, c0 : c0 + MB, :].rearrange("b m s -> m b s"), in_=o_q[:, blk, :, :]
+            )
+
+        A = [0, 1, 2, 3]
+        for g in range(G):
+            for bk in A:
+                pass_x(g, bk, w_a[g], NB * bk)
+        leave_1(A, 0)
+        for g in (0, 1):
+            for bk in (4, 5, 6):
+                pass_x(g, bk, w_b[g], NB * (bk - 4))
+        leave_2(A)
+        leave_3(A, 0)
+        for g in (2, 3):
+            for bk in (4, 5, 6):
+                pass_x(g, bk, w_b[g], NB * (bk - 4))
+        for blk in range(4):
+            acc_q[blk] = psum.tile([P, TOK], F32, name="accq%d" % blk, tag="bank%d" % Q_BANK[blk])
+            for g in range(FULL_G):
+                c0 = 3 * NB + MB * blk
+                pass_w(g, blk, w_b[g][:, c0 : c0 + MB])
+        for g in range(FULL_G, G):
+            for bk in (4, 5):
+                pass_x(g, bk, w_45[g - FULL_G], NB * (bk - 4))
+        leave_1([4, 5], 0)
+        for g in (4, 5):
+            pass_x(g, 6, w_6[g - FULL_G], 0)
+        leave_2([4, 5])
+        leave_3([4, 5], 0)
+        for g in (6, 7):
+            pass_x(g, 6, w_6[g - FULL_G], 0)
+        leave_1([6], 0)
+        leave_2([6])
+        leave_3([6], 0)
+        engine_of_block = [1, 1, 0, 1]
+        for t, first, nblk in w_q:
+            for i in range(nblk):
+                for g in range(FULL_G, G):
+                    pass_w(g, first + i, t[:, g - FULL_G, MB * i : MB * i + MB])
+            for i in range(nblk):
+                leave_q(first + i, engine_of_block[first + i])

@@ -29,7 +29,6 @@ def tile_simpleconvolution_w_kernel(tc, x, weight_words, weight_scales, out):
     with ExitStack() as ctx:
         keep = ctx.enter_context(tc.tile_pool(name="keep", bufs=1))
         psum = ctx.enter_context(tc.psum_pool(name="ps", bufs=1))
-        ctx.enter_context(tc.manual_schedule())
 
         planes = []
         for c in range(2):

from contextlib import ExitStack

import concourse.mybir as mybir
from concourse.masks import make_identity

F32 = mybir.dt.float32
BF16 = mybir.dt.bfloat16
I32 = mybir.dt.int32
U32 = mybir.dt.uint32
U8 = mybir.dt.uint8
FP8X4 = mybir.dt.float8_e4m3fn_x4

P = 128
G = 8
NB = 512
TOK = 128
COUT = 4096
MB = 128
FLOPS = 2 * TOK * 4096 * COUT

FULL_G = 4
XS_BANKS = [0, 1, 2, 3, 4, 5, 6]
Q0 = NB * 7
Q_BANK = [7, 0, 1, 2]


def tile_simpleconvolution_w_kernel(tc, x, weight_words, weight_scales, out):
    nc = tc.nc
    with ExitStack() as ctx:
        keep = ctx.enter_context(tc.tile_pool(name="keep", bufs=1))
        psum = ctx.enter_context(tc.psum_pool(name="ps", bufs=1))

        planes = []
        for c in range(2):
            pl = keep.tile([P, COUT], U8, name="planes%d" % c, align_bytes=64)
            nc.vector.memset(pl[:].bitcast(I32), 0)
            planes.append(pl)

        xr = keep.tile([P, 2, 2048], BF16, name="xr")
        nc.sync.dma_start(out=xr[:], in_=x.rearrange("b (q i) h w -> q b (i h w)", i=32))

        ident = keep.tile([P, P], F32, name="ident")
        make_identity(nc, ident[:])

        for c in range(2):
            for q in range(4):
                nc.gpsimd.dma_start(
                    out=planes[c][32 * q : 32 * q + 16, :].bitcast(F32),
                    in_=weight_scales[4 * c : 4 * c + 4, 4 * q : 4 * q + 4, :].bitcast(F32),
                )

        def load(g, c0, c1):
            t = keep.tile([P, c1 - c0], I32, name="w%d_%d" % (g, c0), align_bytes=64)
            src = weight_words[g].rearrange("p n t -> p (n t)")[:, 4 * c0 : 4 * c1]
            nc.sync.dma_start(out=t[:], in_=src.bitcast(I32))
            return t

        w_a = [load(g, 0, 4 * NB) for g in range(G)]
        w_b = [load(g, 4 * NB, COUT) for g in range(FULL_G)]
        w_45 = [load(g, 4 * NB, 6 * NB) for g in range(FULL_G, G)]
        w_6 = [load(g, 6 * NB, 7 * NB) for g in range(FULL_G, G)]
        w_q = []
        for first, nblk in ((0, 2), (2, 1), (3, 1)):
            c0 = Q0 + MB * first
            t = keep.tile([P, G - FULL_G, MB * nblk], I32, name="wq%d" % first, align_bytes=64)
            src = weight_words[FULL_G:G].rearrange("g p n t -> p g (n t)")[:, :, 4 * c0 : 4 * (c0 + MB * nblk)]
            nc.sync.dma_start(out=t[:], in_=src.bitcast(I32))
            w_q.append((t, first, nblk))

        grouped = keep.tile([P, G, TOK, 4], BF16, name="grouped", align_bytes=64)
        x_codes = keep.tile([P, G * TOK], U32, name="x_codes", align_bytes=64)
        x_plane = keep.tile([P, G * TOK], U8, name="x_plane", align_bytes=64)

        def copy_on(e, dst, src):
            if e % 2 == 0:
                nc.vector.tensor_copy(out=dst, in_=src)
            else:
                nc.scalar.copy(out=dst, in_=src)

        xw = xr[:].bitcast(F32)
        turned = keep.tile([P, 2, P, 8], F32, name="turned")
        for b in range(2):
            for half in range(2):
                t1 = psum.tile([P, 4, P], F32, name="t1_%d%d" % (b, half), tag="bank%d" % (2 * b + half))
                for i in range(4):
                    c0 = P * (4 * half + i)
                    nc.tensor.transpose(t1[:, i, :], xw[:, b, c0 : c0 + P], ident[:])
                copy_on(
                    b, turned[:, b, :, 4 * half : 4 * half + 4], t1[:].rearrange("c i q -> c q i")
                )
        for b in range(2):
            for half in range(2):
                t2 = psum.tile([P, 4, P], F32, name="t2_%d%d" % (b, half), tag="bank%d" % (4 + 2 * b + half))
                for i in range(4):
                    g = 4 * half + i
                    nc.tensor.transpose(
                        t2[:, i, :],
                        turned[:, b, 16 * g : 16 * g + 16, :].rearrange("c h l -> c (h l)"),
                        ident[:],
                    )
                copy_on(
                    b,
                    grouped[:, 4 * half : 4 * half + 4, 64 * b : 64 * b + 64, :],
                    t2[:].bitcast(BF16).rearrange("p g (t s) -> p g s t", t=4),
                )
        nc.vector.quantize_mx(
            out=x_codes[:].bitcast(FP8X4),
            scales=x_plane[:],
            in_=grouped[:].rearrange("p g k t -> p (g k t)"),
        )

        out_f = out.rearrange("b o h w -> b o (h w)")

        acc = {}
        for bk in XS_BANKS:
            acc[bk] = psum.tile([P, NB], F32, name="acc%d" % bk, tag="bank%d" % bk)

        def pass_x(g, bk, wt, col):
            k = 4 * (g % 4)
            nc.tensor.matmul_mx(
                out=acc[bk][:],
                lhsT=x_codes[:, TOK * g : TOK * g + TOK].bitcast(FP8X4),
                lhsT_scale=x_plane[:, TOK * g : TOK * g + TOK],
                rhs=wt[:, col : col + NB].bitcast(FP8X4),
                rhs_scale=planes[g // 4][k:P, NB * bk : NB * bk + NB],
                start=(g == 0),
                stop=(g == G - 1),
            )

        acc_q = {}

        def pass_w(g, blk, w_ap):
            k = 4 * (g % 4)
            c0 = Q0 + MB * blk
            nc.tensor.matmul_mx(
                out=acc_q[blk][:],
                lhsT=w_ap.bitcast(FP8X4),
                lhsT_scale=planes[g // 4][k:P, c0 : c0 + MB],
                rhs=x_codes[:, TOK * g : TOK * g + TOK].bitcast(FP8X4),
                rhs_scale=x_plane[:, TOK * g : TOK * g + TOK],
                start=(g == 0),
                stop=(g == G - 1),
            )

        s1 = {}
        tp = {}

        def leave_1(grp, e):
            nb = len(grp)
            jg = 4 * nb
            mc = P // nb
            s1[grp[0]] = keep.tile([P, jg, P], F32, name="s1_%d" % grp[0])
            for i, bk in enumerate(grp):
                copy_on(
                    e + i,
                    s1[grp[0]][:, :, mc * i : mc * i + mc],
                    acc[bk][:].rearrange("p (m j) -> p j m", j=jg),
                )

        def leave_2(grp):
            for i, bk in enumerate(grp):
                tp[bk] = psum.tile([P, 4, TOK], F32, name="tp%d" % bk, tag="bank%d" % bk)
                for j in range(4):
                    nc.tensor.transpose(tp[bk][:, j, :], s1[grp[0]][:, 4 * i + j, :], ident[:])

        def leave_3(grp, e):
            jg = 4 * len(grp)
            o_sb = keep.tile([P, 2, jg, 64], F32, name="o_%d" % grp[0])
            for i, bk in enumerate(grp):
                copy_on(
                    e + i,
                    o_sb[:, :, 4 * i : 4 * i + 4, :],
                    tp[bk][:].rearrange("p j (b s) -> p b j s", b=2),
                )
            base = NB * grp[0]
            nc.sync.dma_start(
                out=out_f[:, base : base + NB * len(grp), :].rearrange("b (m j) s -> m b (j s)", j=jg),
                in_=o_sb[:].rearrange("p b j s -> p b (j s)"),
            )

        o_q = keep.tile([P, 4, 2, 64], F32, name="o_q")

        def leave_q(blk, e):
            copy_on(e, o_q[:, blk, :, :].rearrange("p b s -> p (b s)"), acc_q[blk][:])
            c0 = Q0 + MB * blk
            nc.sync.dma_start(
                out=out_f[:, c0 : c0 + MB, :].rearrange("b m s -> m b s"), in_=o_q[:, blk, :, :]
            )

        A = [0, 1, 2, 3]
        for g in range(G):
            for bk in A:
                pass_x(g, bk, w_a[g], NB * bk)
        leave_1(A, 0)
        for g in (0, 1):
            for bk in (4, 5, 6):
                pass_x(g, bk, w_b[g], NB * (bk - 4))
        leave_2(A)
        leave_3(A, 0)
        for g in (2, 3):
            for bk in (4, 5, 6):
                pass_x(g, bk, w_b[g], NB * (bk - 4))
        for blk in range(4):
            acc_q[blk] = psum.tile([P, TOK], F32, name="accq%d" % blk, tag="bank%d" % Q_BANK[blk])
            for g in range(FULL_G):
                c0 = 3 * NB + MB * blk
                pass_w(g, blk, w_b[g][:, c0 : c0 + MB])
        for g in range(FULL_G, G):
            for bk in (4, 5):
                pass_x(g, bk, w_45[g - FULL_G], NB * (bk - 4))
        leave_1([4, 5], 0)
        for g in (4, 5):
            pass_x(g, 6, w_6[g - FULL_G], 0)
        leave_2([4, 5])
        leave_3([4, 5], 0)
        for g in (6, 7):
            pass_x(g, 6, w_6[g - FULL_G], 0)
        leave_1([6], 0)
        leave_2([6])
        leave_3([6], 0)
        engine_of_block = [1, 1, 0, 1]
        for t, first, nblk in w_q:
            for i in range(nblk):
                for g in range(FULL_G, G):
                    pass_w(g, first + i, t[:, g - FULL_G, MB * i : MB * i + MB])
            for i in range(nblk):
                leave_q(first + i, engine_of_block[first + i])
